import numpy as np
import ml_dtypes


def mxq(x, axis, fmt="e4m3"):
    dtype, down = {"e4m3": (ml_dtypes.float8_e4m3fn, 7), "e5m2": (ml_dtypes.float8_e5m2, 14)}[fmt]
    v = np.moveaxis(np.asarray(x, np.float32).astype(ml_dtypes.bfloat16).astype(np.float64), axis, -1)
    blocks = v.reshape(v.shape[:-1] + (-1, 32))
    amax = np.abs(blocks).max(-1, keepdims=True)
    byte = np.maximum(np.where(amax > 0, np.frexp(amax)[1] - 1 + 127, 0) - down, 1)
    scale = np.exp2(byte - 127.0)
    codes = (blocks / scale).astype(np.float32).astype(dtype).astype(np.float64)
    return np.moveaxis((codes * scale).reshape(v.shape), -1, axis)


WIDE = False


def mx_kscale(k):
    if not WIDE:
        return np.ones(k)
    levels = np.array([20, -20, 10, -10, 0])
    a = np.random.permutation(np.resize(levels, k // 512 * 4)).reshape(k // 512, 4)
    idx = np.arange(k)
    return np.exp2(a[idx // 512, idx % 128 // 32])


BF16 = ml_dtypes.bfloat16


def bf(x):
    return np.asarray(x, np.float32).astype(BF16)


def f64(x):
    return np.asarray(x).astype(np.float64)


N, NQ, G, KW = 1024, 512, 3, 3
P = KW - 1
T = G * N


def rows(q):
    return q.transpose(2, 0, 1).reshape(T, NQ)


def taps(x, q2):
    xt = x.reshape(N, NQ, G, P).transpose(3, 2, 0, 1).reshape(P, T, NQ)
    return np.concatenate([xt, rows(q2)[None]], 0)


def preact(x, q2, q1, W3, b3):
    y = (taps(x, q2) @ W3.transpose(2, 1, 0)).sum(0) + b3
    return y.reshape(G, N, NQ).transpose(1, 2, 0) + q1


def setup_inputs():
    s = mx_kscale(T).reshape(G, N).T[:, None, :]
    w = 1.0 / np.sqrt(KW * NQ)
    x0 = bf(np.random.standard_normal((N, NQ, G * P)))
    q20 = bf(np.maximum(np.random.standard_normal((N, NQ, G)) * 0.9, 0.0))
    q1 = bf(np.random.standard_normal((N, NQ, G)))
    W3 = bf(np.random.standard_normal((NQ, NQ, KW)) * w)
    b3 = bf(np.random.standard_normal(NQ) * 0.2)
    g = bf(np.random.standard_normal((N, NQ, G)) * np.exp2(np.random.randint(-12, 1, (N, 1, G))) / s)
    z = preact(f64(x0), f64(q20), f64(q1), f64(W3), f64(b3))
    return {"x": bf(f64(x0) * np.repeat(s, P, axis=2)), "q2": bf(f64(q20) * s), "q1": q1, "W3": W3, "b3": b3,
            "z": np.asarray(z, np.float32), "grad_out": g}


def reference(x, q2, q1, W3, b3, z, grad_out):
    dz = f64(grad_out) * (f64(z) > 0.0)
    dq = mxq(rows(dz), 0, "e5m2")
    tq = mxq(taps(f64(x), f64(q2)), 1, "e4m3")
    return (tq.swapaxes(1, 2) @ dq).transpose(2, 1, 0)

@@ -1,0 +1,161 @@
+from contextlib import ExitStack
+
+import concourse.mybir as mybir
+
+BF16 = mybir.dt.bfloat16
+F32 = mybir.dt.float32
+U32 = mybir.dt.uint32
+U8 = mybir.dt.uint8
+E4M3X4 = mybir.dt.float8_e4m3fn_x4
+E5M2X4 = mybir.dt.float8_e5m2_x4
+
+P = 128
+PACK = 4
+K_PASS = P * PACK
+N, NQ, G, TAPS = 1024, 512, 3, 3
+HALVES = N // K_PASS
+COLS = NQ * TAPS
+N_TILE = 512
+SLICES = COLS // N_TILE
+C_PIECE = 256
+O_CHUNK = P
+O_CHUNKS = NQ // O_CHUNK
+VECTOR_C = 128
+WIDEST_QUANTISE = 2048
+
+FLOPS = 2 * N * G * NQ * COLS
+BYTES = 2 * N * NQ * (2 * G + G + G) + 4 * N * NQ * G + 4 * NQ * COLS
+
+
+def power_of_two_cuts(total):
+    cuts = []
+    start = 0
+    width = WIDEST_QUANTISE
+    while start < total:
+        if width <= total - start:
+            cuts.append((start, width))
+            start += width
+        else:
+            width //= 2
+    return cuts
+
+
+def tile_quadjetresnetblock_pb_v_kernel(tc, x, q2, q1, W3, b3, z, grad_out, out):
+    nc = tc.nc
+    out_rows = out.rearrange("o c t -> o (c t)")
+
+    with ExitStack() as ctx:
+        keep = ctx.enter_context(tc.tile_pool(name="keep", bufs=1))
+        taps_raw = ctx.enter_context(tc.tile_pool(name="taps_raw", bufs=3))
+        taps_grouped = ctx.enter_context(tc.tile_pool(name="taps_grouped", bufs=6))
+        dz_raw = ctx.enter_context(tc.tile_pool(name="dz_raw", bufs=5))
+        dz_grouped = ctx.enter_context(tc.tile_pool(name="dz_grouped", bufs=3))
+        results = ctx.enter_context(tc.tile_pool(name="results", bufs=6))
+        psum = ctx.enter_context(tc.psum_pool(name="psum", bufs=2))
+
+        tap_codes = keep.tile([P, HALVES, G, COLS], U32, align_bytes=64)
+        tap_scales = keep.tile([P, HALVES, G, COLS], U8, align_bytes=64)
+        dz_codes = keep.tile([P, HALVES, O_CHUNKS, G * O_CHUNK], U32, align_bytes=64)
+        dz_scales = keep.tile([P, HALVES, O_CHUNKS, G * O_CHUNK], U8, align_bytes=64)
+
+        def quantise(grouped_flat, codes, scales, x4):
+            for start, width in power_of_two_cuts(grouped_flat.shape[1]):
+                words = slice(start // PACK, (start + width) // PACK)
+                nc.vector.quantize_mx(
+                    out=codes[:, words].bitcast(x4),
+                    scales=scales[:, words],
+                    in_=grouped_flat[:, start : start + width],
+                )
+
+        def make_taps(h, piece):
+            n_rows = slice(h * K_PASS, (h + 1) * K_PASS)
+            chans = slice(piece * C_PIECE, (piece + 1) * C_PIECE)
+            cols = slice(piece * C_PIECE * TAPS, (piece + 1) * C_PIECE * TAPS)
+            x_raw = taps_raw.tile([P, PACK, C_PIECE, 2 * G], BF16)
+            nc.sync.dma_start(out=x_raw[:], in_=x[n_rows, chans, :].rearrange("(p j) c s -> p j c s", j=PACK))
+            q2_raw = taps_raw.tile([P, PACK, C_PIECE, G], BF16)
+            nc.sync.dma_start(out=q2_raw[:], in_=q2[n_rows, chans, :].rearrange("(p j) c s -> p j c s", j=PACK))
+            for g in range(G):
+                grouped = taps_grouped.tile([P, C_PIECE, TAPS, PACK], BF16, align_bytes=64)
+                for copy, c_range in (
+                    (nc.vector.tensor_copy, slice(0, VECTOR_C)),
+                    (nc.scalar.copy, slice(VECTOR_C, C_PIECE)),
+                ):
+                    copy(
+                        out=grouped[:, c_range, 0:2, :].rearrange("p c k j -> p c j k"),
+                        in_=x_raw[:, :, c_range, 2 * g : 2 * g + 2].rearrange("p j c k -> p c j k"),
+                    )
+                    copy(
+                        out=grouped[:, c_range, 2, :],
+                        in_=q2_raw[:, :, c_range, g].rearrange("p j c -> p c j"),
+                    )
+                quantise(
+                    grouped[:].rearrange("p c t j -> p (c t j)"),
+                    tap_codes[:, h, g, cols],
+                    tap_scales[:, h, g, cols],
+                    E4M3X4,
+                )
+
+        def make_dz(h, oc):
+            n_rows = slice(h * K_PASS, (h + 1) * K_PASS)
+            chans = slice(oc * O_CHUNK, (oc + 1) * O_CHUNK)
+            z_raw = dz_raw.tile([P, PACK, O_CHUNK, G], F32)
+            nc.sync.dma_start(out=z_raw[:], in_=z[n_rows, chans, :].rearrange("(p j) o g -> p j o g", j=PACK))
+            grad_raw = dz_raw.tile([P, PACK, O_CHUNK, G], BF16)
+            nc.sync.dma_start(
+                out=grad_raw[:], in_=grad_out[n_rows, chans, :].rearrange("(p j) o g -> p j o g", j=PACK)
+            )
+            grouped = dz_grouped.tile([P, G, O_CHUNK, PACK], BF16, align_bytes=64)
+            for g in range(G):
+                nc.vector.scalar_tensor_tensor(
+                    out=grouped[:, g, :, :],
+                    in0=z_raw[:, :, :, g].rearrange("p j o -> p o j"),
+                    scalar=0.0,
+                    in1=grad_raw[:, :, :, g].rearrange("p j o -> p o j"),
+                    op0=mybir.AluOpType.is_gt,
+                    op1=mybir.AluOpType.mult,
+                )
+            quantise(
+                grouped[:].rearrange("p g o j -> p (g o j)"), dz_codes[:, h, oc, :], dz_scales[:, h, oc, :], E5M2X4
+            )
+
+        def multiply(h, oc, banks):
+            for g in range(G):
+                o_words = slice(g * O_CHUNK, (g + 1) * O_CHUNK)
+                for s in range(SLICES):
+                    cols = slice(s * N_TILE, (s + 1) * N_TILE)
+                    nc.tensor.matmul_mx(
+                        out=banks[s][:],
+                        lhsT=dz_codes[:, h, oc, o_words].bitcast(E5M2X4),
+                        lhsT_scale=dz_scales[:, h, oc, o_words],
+                        rhs=tap_codes[:, h, g, cols].bitcast(E4M3X4),
+                        rhs_scale=tap_scales[:, h, g, cols],
+                        start=(h == 0 and g == 0),
+                        stop=(h == HALVES - 1 and g == G - 1),
+                    )
+
+        def new_banks():
+            return [psum.tile([P, N_TILE], F32, name="bank%d" % s) for s in range(SLICES)]
+
+        def store(oc, banks):
+            for s in range(SLICES):
+                result = results.tile([P, N_TILE], F32)
+                nc.scalar.copy(out=result[:], in_=banks[s][:])
+                nc.scalar.dma_start(
+                    out=out_rows[oc * O_CHUNK : (oc + 1) * O_CHUNK, s * N_TILE : (s + 1) * N_TILE], in_=result[:]
+                )
+
+        for h in range(HALVES):
+            for piece in range(NQ // C_PIECE):
+                make_taps(h, piece)
+        for oc in range(O_CHUNKS):
+            make_dz(0, oc)
+        banks = {0: new_banks()}
+        multiply(0, 0, banks[0])
+        for oc in range(O_CHUNKS):
+            if oc + 1 < O_CHUNKS:
+                banks[oc + 1] = new_banks()
+                multiply(0, oc + 1, banks[oc + 1])
+            make_dz(1, oc)
+            multiply(1, oc, banks[oc])
+            store(oc, banks[oc])

@@ -105,16 +105,19 @@ def tile_quadjetresnetblock_pb_v_kernel(tc, x, q2, q1, W3, b3, z, grad_out, out)
             nc.sync.dma_start(
                 out=grad_raw[:], in_=grad_out[n_rows, chans, :].rearrange("(p j) o g -> p j o g", j=PACK)
             )
+            dz_rows = dz_grouped.tile([P, PACK, O_CHUNK, G], BF16)
+            nc.vector.scalar_tensor_tensor(
+                out=dz_rows[:].rearrange("p j o g -> p (j o g)"),
+                in0=z_raw[:].rearrange("p j o g -> p (j o g)"),
+                scalar=0.0,
+                in1=grad_raw[:].rearrange("p j o g -> p (j o g)"),
+                op0=mybir.AluOpType.is_gt,
+                op1=mybir.AluOpType.mult,
+            )
             grouped = dz_grouped.tile([P, G, O_CHUNK, PACK], BF16, align_bytes=64)
-            for g in range(G):
-                nc.vector.scalar_tensor_tensor(
-                    out=grouped[:, g, :, :],
-                    in0=z_raw[:, :, :, g].rearrange("p j o -> p o j"),
-                    scalar=0.0,
-                    in1=grad_raw[:, :, :, g].rearrange("p j o -> p o j"),
-                    op0=mybir.AluOpType.is_gt,
-                    op1=mybir.AluOpType.mult,
-                )
+            nc.scalar.copy(
+                out=grouped[:].rearrange("p g o j -> p o j g"), in_=dz_rows[:].rearrange("p j o g -> p o j g")
+            )
             quantise(
                 grouped[:].rearrange("p g o j -> p (g o j)"), dz_codes[:, h, oc, :], dz_scales[:, h, oc, :], E5M2X4
             )

@@ -20,7 +20,8 @@ SLICES = COLS // N_TILE
 C_PIECE = 256
 O_CHUNK = P
 O_CHUNKS = NQ // O_CHUNK
-VECTOR_C = 128
+EARLY_CHUNKS = 2
+VECTOR_C = 144
 WIDEST_QUANTISE = 2048
 
 FLOPS = 2 * N * G * NQ * COLS
@@ -122,43 +123,52 @@ def tile_quadjetresnetblock_pb_v_kernel(tc, x, q2, q1, W3, b3, z, grad_out, out)
                 grouped[:].rearrange("p g o j -> p (g o j)"), dz_codes[:, h, oc, :], dz_scales[:, h, oc, :], E5M2X4
             )
 
-        def multiply(h, oc, banks):
+        def multiply(h, oc, s, bank):
+            cols = slice(s * N_TILE, (s + 1) * N_TILE)
             for g in range(G):
                 o_words = slice(g * O_CHUNK, (g + 1) * O_CHUNK)
-                for s in range(SLICES):
-                    cols = slice(s * N_TILE, (s + 1) * N_TILE)
-                    nc.tensor.matmul_mx(
-                        out=banks[s][:],
-                        lhsT=dz_codes[:, h, oc, o_words].bitcast(E5M2X4),
-                        lhsT_scale=dz_scales[:, h, oc, o_words],
-                        rhs=tap_codes[:, h, g, cols].bitcast(E4M3X4),
-                        rhs_scale=tap_scales[:, h, g, cols],
-                        start=(h == 0 and g == 0),
-                        stop=(h == HALVES - 1 and g == G - 1),
-                    )
+                nc.tensor.matmul_mx(
+                    out=bank[:],
+                    lhsT=dz_codes[:, h, oc, o_words].bitcast(E5M2X4),
+                    lhsT_scale=dz_scales[:, h, oc, o_words],
+                    rhs=tap_codes[:, h, g, cols].bitcast(E4M3X4),
+                    rhs_scale=tap_scales[:, h, g, cols],
+                    start=(h == 0 and g == 0),
+                    stop=(h == HALVES - 1 and g == G - 1),
+                )
+
+        def store(oc, s, bank):
+            result = results.tile([P, N_TILE], F32)
+            nc.scalar.copy(out=result[:], in_=bank[:])
+            nc.scalar.dma_start(
+                out=out_rows[oc * O_CHUNK : (oc + 1) * O_CHUNK, s * N_TILE : (s + 1) * N_TILE], in_=result[:]
+            )
 
         def new_banks():
             return [psum.tile([P, N_TILE], F32, name="bank%d" % s) for s in range(SLICES)]
 
-        def store(oc, banks):
+        def finish(oc, banks):
             for s in range(SLICES):
-                result = results.tile([P, N_TILE], F32)
-                nc.scalar.copy(out=result[:], in_=banks[s][:])
-                nc.scalar.dma_start(
-                    out=out_rows[oc * O_CHUNK : (oc + 1) * O_CHUNK, s * N_TILE : (s + 1) * N_TILE], in_=result[:]
-                )
+                multiply(1, oc, s, banks[s])
+                store(oc, s, banks[s])
 
-        for h in range(HALVES):
-            for piece in range(NQ // C_PIECE):
-                make_taps(h, piece)
-        for oc in range(O_CHUNKS):
+        for piece in range(NQ // C_PIECE):
+            make_taps(0, piece)
+        early_banks = []
+        for oc in range(EARLY_CHUNKS):
+            early_banks.append(new_banks())
             make_dz(0, oc)
-        banks = {0: new_banks()}
-        multiply(0, 0, banks[0])
-        for oc in range(O_CHUNKS):
-            if oc + 1 < O_CHUNKS:
-                banks[oc + 1] = new_banks()
-                multiply(0, oc + 1, banks[oc + 1])
             make_dz(1, oc)
-            multiply(1, oc, banks[oc])
-            store(oc, banks[oc])
+            for s in range(SLICES):
+                multiply(0, oc, s, early_banks[oc][s])
+        for piece in range(NQ // C_PIECE):
+            make_taps(1, piece)
+        for oc in range(EARLY_CHUNKS):
+            finish(oc, early_banks[oc])
+        for oc in range(EARLY_CHUNKS, O_CHUNKS):
+            banks = new_banks()
+            make_dz(0, oc)
+            for s in range(SLICES):
+                multiply(0, oc, s, banks[s])
+            make_dz(1, oc)
+            finish(oc, banks)

@@ -17,12 +17,23 @@ HALVES = N // K_PASS
 COLS = NQ * TAPS
 N_TILE = 512
 SLICES = COLS // N_TILE
-C_PIECE = 256
+WIDE = 256
+QUAD = 4
+QUAD_COLS = QUAD * TAPS
 O_CHUNK = P
 O_CHUNKS = NQ // O_CHUNK
-EARLY_CHUNKS = 2
-VECTOR_C = 144
 WIDEST_QUANTISE = 2048
+
+BANKS = 8
+BANK_BUFS = 8
+WIDEST_PIECE = 256
+DRAIN = 2
+V_SHARE = (512, 512, 256)
+RAW_BUFS = 6
+V_DZ = {(h, oc): 0 for h in range(2) for oc in range(4)}
+STEPS = (("T", 0, 0, 64), ("T", 0, 64, 192), ("T", 0, 256, 256), ("Z", 0, 0), ("Z", 0, 1), ("T", 1, 0, 256), ("T", 1, 256, 256), ("Z", 1, 0), ("Z", 1, 1), ("Z", 0, 2), ("Z", 0, 3), ("Z", 1, 2), ("Z", 1, 3))
+LOADS = ((0, ("T", 0, 0, 64)), (0, ("T", 0, 64, 192)), (0, ("T", 0, 256, 256)), (0, ("Z", 0, 0, 256)), (0, ("T", 1, 0, 256)), (0, ("T", 1, 256, 256)), (0, ("Z", 1, 0, 256)), (2, ("Z", 0, 256, 256)), (3, ("Z", 1, 256, 128)), (3, ("Z", 1, 384, 128)))
+V_EMPTIES = (1,)
 
 FLOPS = 2 * N * G * NQ * COLS
 BYTES = 2 * N * NQ * (2 * G + G + G) + 4 * N * NQ * G + 4 * NQ * COLS
@@ -47,17 +58,21 @@ def tile_quadjetresnetblock_pb_v_kernel(tc, x, q2, q1, W3, b3, z, grad_out, out)
 
     with ExitStack() as ctx:
         keep = ctx.enter_context(tc.tile_pool(name="keep", bufs=1))
-        taps_raw = ctx.enter_context(tc.tile_pool(name="taps_raw", bufs=3))
-        taps_grouped = ctx.enter_context(tc.tile_pool(name="taps_grouped", bufs=6))
-        dz_raw = ctx.enter_context(tc.tile_pool(name="dz_raw", bufs=5))
-        dz_grouped = ctx.enter_context(tc.tile_pool(name="dz_grouped", bufs=3))
-        results = ctx.enter_context(tc.tile_pool(name="results", bufs=6))
-        psum = ctx.enter_context(tc.psum_pool(name="psum", bufs=2))
+        taps_grouped = ctx.enter_context(tc.tile_pool(name="taps_grouped", bufs=3))
+        raw = ctx.enter_context(tc.tile_pool(name="raw", bufs=RAW_BUFS))
+        dz_work = ctx.enter_context(tc.tile_pool(name="dz_work", bufs=2))
+        psum = ctx.enter_context(tc.psum_pool(name="psum", bufs=BANK_BUFS))
+        ctx.enter_context(tc.manual_schedule())
 
         tap_codes = keep.tile([P, HALVES, G, COLS], U32, align_bytes=64)
         tap_scales = keep.tile([P, HALVES, G, COLS], U8, align_bytes=64)
         dz_codes = keep.tile([P, HALVES, O_CHUNKS, G * O_CHUNK], U32, align_bytes=64)
         dz_scales = keep.tile([P, HALVES, O_CHUNKS, G * O_CHUNK], U8, align_bytes=64)
+        result = [keep.tile([P, COLS], F32, name="result%d" % oc) for oc in range(O_CHUNKS)]
+
+        def rows_of(src, h, first, width):
+            n_rows = slice(h * K_PASS, (h + 1) * K_PASS)
+            return src[n_rows, first : first + width, :].rearrange("(p j) c s -> p j c s", j=PACK)
 
         def quantise(grouped_flat, codes, scales, x4):
             for start, width in power_of_two_cuts(grouped_flat.shape[1]):
@@ -68,107 +83,187 @@ def tile_quadjetresnetblock_pb_v_kernel(tc, x, q2, q1, W3, b3, z, grad_out, out)
                     in_=grouped_flat[:, start : start + width],
                 )
 
-        def make_taps(h, piece):
-            n_rows = slice(h * K_PASS, (h + 1) * K_PASS)
-            chans = slice(piece * C_PIECE, (piece + 1) * C_PIECE)
-            cols = slice(piece * C_PIECE * TAPS, (piece + 1) * C_PIECE * TAPS)
-            x_raw = taps_raw.tile([P, PACK, C_PIECE, 2 * G], BF16)
-            nc.sync.dma_start(out=x_raw[:], in_=x[n_rows, chans, :].rearrange("(p j) c s -> p j c s", j=PACK))
-            q2_raw = taps_raw.tile([P, PACK, C_PIECE, G], BF16)
-            nc.sync.dma_start(out=q2_raw[:], in_=q2[n_rows, chans, :].rearrange("(p j) c s -> p j c s", j=PACK))
-            for g in range(G):
-                grouped = taps_grouped.tile([P, C_PIECE, TAPS, PACK], BF16, align_bytes=64)
-                for copy, c_range in (
-                    (nc.vector.tensor_copy, slice(0, VECTOR_C)),
-                    (nc.scalar.copy, slice(VECTOR_C, C_PIECE)),
-                ):
-                    copy(
-                        out=grouped[:, c_range, 0:2, :].rearrange("p c k j -> p c j k"),
-                        in_=x_raw[:, :, c_range, 2 * g : 2 * g + 2].rearrange("p j c k -> p c j k"),
+        tiles = {}
+
+        def load(kind, h, first, width):
+            if first % WIDE == 0:
+                if kind == "T":
+                    tiles[kind, h, first // WIDE] = (
+                        raw.tile([P, PACK, WIDE, 2 * G], BF16, name="raw_wide"),
+                        raw.tile([P, PACK, WIDE, G], BF16, name="raw_narrow"),
                     )
-                    copy(
-                        out=grouped[:, c_range, 2, :],
-                        in_=q2_raw[:, :, c_range, g].rearrange("p j c -> p c j"),
+                else:
+                    tiles[kind, h, first // WIDE] = (
+                        raw.tile([P, PACK, WIDE, G], F32, name="raw_wide"),
+                        raw.tile([P, PACK, WIDE, G], BF16, name="raw_narrow"),
                     )
-                quantise(
-                    grouped[:].rearrange("p c t j -> p (c t j)"),
+            here = slice(first % WIDE, first % WIDE + width)
+            for tile, src in zip(tiles[kind, h, first // WIDE], (x, q2) if kind == "T" else (z, grad_out)):
+                nc.sync.dma_start(out=tile[:, :, here, :], in_=rows_of(src, h, first, width))
+
+        waiting = []
+        closed = []
+
+        def tap_unit(h, first, width, g):
+            x_raw, q2_raw = tiles["T", h, first // WIDE]
+            lo = first % WIDE
+            chans = slice(lo, lo + width)
+            grouped = taps_grouped.tile([P, WIDEST_PIECE // QUAD, TAPS, QUAD, PACK], BF16, align_bytes=64, name="grouped")[:, : width // QUAD]
+            nc.scalar.copy(
+                out=grouped[:, :, 2, :, :].rearrange("p q c j -> p q j c"),
+                in_=q2_raw[:, :, chans, g].rearrange("p j (q c) -> p q j c", c=QUAD),
+            )
+            cut = V_SHARE[g] * width // 512 // (2 * QUAD) * 2
+            if cut:
+                nc.vector.tensor_copy(
+                    out=grouped[:, :cut, 0:2, :, :].rearrange("p q t c j -> p q j c t"),
+                    in_=x_raw[:, :, lo : lo + cut * QUAD, 2 * g : 2 * g + 2].rearrange("p j (q c) t -> p q j c t", c=QUAD),
+                )
+            if cut * QUAD < width:
+                for t in range(2):
+                    nc.scalar.copy(
+                        out=grouped[:, cut:, t, :, :].rearrange("p q c j -> p q j c"),
+                        in_=x_raw[:, :, lo + cut * QUAD : lo + width, 2 * g + t].rearrange("p j (q c) -> p q j c", c=QUAD),
+                    )
+            cols = slice(first * TAPS, (first + width) * TAPS)
+            waiting.append((
+                ("T", h, first + width, g),
+                lambda: quantise(
+                    grouped.rearrange("p q t c j -> p (q t c j)"),
                     tap_codes[:, h, g, cols],
                     tap_scales[:, h, g, cols],
                     E4M3X4,
-                )
+                ),
+            ))
 
-        def make_dz(h, oc):
-            n_rows = slice(h * K_PASS, (h + 1) * K_PASS)
-            chans = slice(oc * O_CHUNK, (oc + 1) * O_CHUNK)
-            z_raw = dz_raw.tile([P, PACK, O_CHUNK, G], F32)
-            nc.sync.dma_start(out=z_raw[:], in_=z[n_rows, chans, :].rearrange("(p j) o g -> p j o g", j=PACK))
-            grad_raw = dz_raw.tile([P, PACK, O_CHUNK, G], BF16)
-            nc.sync.dma_start(
-                out=grad_raw[:], in_=grad_out[n_rows, chans, :].rearrange("(p j) o g -> p j o g", j=PACK)
-            )
-            dz_rows = dz_grouped.tile([P, PACK, O_CHUNK, G], BF16)
+        def dz_unit(h, oc):
+            z_raw, grad_raw = tiles["Z", h, oc * O_CHUNK // WIDE]
+            first = oc * O_CHUNK % WIDE
+            part = slice(first, first + O_CHUNK)
+            dz_rows = dz_work.tile([P, PACK, O_CHUNK, G], BF16, name="dz_rows")
             nc.vector.scalar_tensor_tensor(
-                out=dz_rows[:].rearrange("p j o g -> p (j o g)"),
-                in0=z_raw[:].rearrange("p j o g -> p (j o g)"),
+                out=dz_rows[:].rearrange("p j o g -> p j (o g)"),
+                in0=z_raw[:, :, part, :].rearrange("p j o g -> p j (o g)"),
                 scalar=0.0,
-                in1=grad_raw[:].rearrange("p j o g -> p (j o g)"),
+                in1=grad_raw[:, :, part, :].rearrange("p j o g -> p j (o g)"),
                 op0=mybir.AluOpType.is_gt,
                 op1=mybir.AluOpType.mult,
             )
-            grouped = dz_grouped.tile([P, G, O_CHUNK, PACK], BF16, align_bytes=64)
-            nc.scalar.copy(
-                out=grouped[:].rearrange("p g o j -> p o j g"), in_=dz_rows[:].rearrange("p j o g -> p o j g")
-            )
-            quantise(
-                grouped[:].rearrange("p g o j -> p (g o j)"), dz_codes[:, h, oc, :], dz_scales[:, h, oc, :], E5M2X4
-            )
+            grouped = dz_work.tile([P, G, O_CHUNK, PACK], BF16, align_bytes=64, name="dz_grouped")
+            for copy, o_range in ((nc.vector.tensor_copy, slice(0, V_DZ[h, oc])), (nc.scalar.copy, slice(V_DZ[h, oc], O_CHUNK))):
+                if o_range.start < o_range.stop:
+                    copy(
+                        out=grouped[:, :, o_range, :].rearrange("p g o j -> p o j g"),
+                        in_=dz_rows[:, :, o_range, :].rearrange("p j o g -> p o j g"),
+                    )
+            waiting.append((
+                ("Z", h, oc),
+                lambda: quantise(
+                    grouped[:].rearrange("p g o j -> p (g o j)"), dz_codes[:, h, oc, :], dz_scales[:, h, oc, :], E5M2X4
+                ),
+            ))
 
-        def multiply(h, oc, s, bank):
+        def multiply(h, oc, s, g, bank):
             cols = slice(s * N_TILE, (s + 1) * N_TILE)
-            for g in range(G):
-                o_words = slice(g * O_CHUNK, (g + 1) * O_CHUNK)
-                nc.tensor.matmul_mx(
-                    out=bank[:],
-                    lhsT=dz_codes[:, h, oc, o_words].bitcast(E5M2X4),
-                    lhsT_scale=dz_scales[:, h, oc, o_words],
-                    rhs=tap_codes[:, h, g, cols].bitcast(E4M3X4),
-                    rhs_scale=tap_scales[:, h, g, cols],
-                    start=(h == 0 and g == 0),
-                    stop=(h == HALVES - 1 and g == G - 1),
-                )
-
-        def store(oc, s, bank):
-            result = results.tile([P, N_TILE], F32)
-            nc.scalar.copy(out=result[:], in_=bank[:])
-            nc.scalar.dma_start(
-                out=out_rows[oc * O_CHUNK : (oc + 1) * O_CHUNK, s * N_TILE : (s + 1) * N_TILE], in_=result[:]
+            o_words = slice(g * O_CHUNK, (g + 1) * O_CHUNK)
+            nc.tensor.matmul_mx(
+                out=bank[:],
+                lhsT=dz_codes[:, h, oc, o_words].bitcast(E5M2X4),
+                lhsT_scale=dz_scales[:, h, oc, o_words],
+                rhs=tap_codes[:, h, g, cols].bitcast(E4M3X4),
+                rhs_scale=tap_scales[:, h, g, cols],
+                start=(h == 0 and g == 0),
+                stop=(h == HALVES - 1 and g == G - 1),
             )
 
-        def new_banks():
-            return [psum.tile([P, N_TILE], F32, name="bank%d" % s) for s in range(SLICES)]
+        def empty(s, bank, result, copy):
+            lo, hi = s * N_TILE, (s + 1) * N_TILE
+            first_quad, last_quad = -(-lo // QUAD_COLS), hi // QUAD_COLS
+            copy(
+                out=result[:, first_quad * QUAD_COLS : last_quad * QUAD_COLS].rearrange("p (q c t) -> p q c t", t=TAPS, c=QUAD),
+                in_=bank[:, first_quad * QUAD_COLS - lo : last_quad * QUAD_COLS - lo].rearrange("p (q t c) -> p q c t", t=TAPS, c=QUAD),
+            )
+            for quad, a, b in ((first_quad - 1, lo, first_quad * QUAD_COLS), (last_quad, last_quad * QUAD_COLS, hi)):
+                if a < b:
+                    start = quad * QUAD_COLS
+                    copy(
+                        out=result[:, start : start + QUAD_COLS].rearrange("p (c t) -> p c t", t=TAPS)[
+                            :, :, (a - start) // QUAD : (b - start) // QUAD
+                        ],
+                        in_=bank[:, a - lo : b - lo].rearrange("p (t c) -> p c t", c=QUAD),
+                    )
 
-        def finish(oc, banks):
-            for s in range(SLICES):
-                multiply(1, oc, s, banks[s])
-                store(oc, s, banks[s])
+        def store(oc, s):
+            a, b = STORE_CUTS[s], STORE_CUTS[s + 1]
+            nc.sync.dma_start(out=out_rows[oc * O_CHUNK : (oc + 1) * O_CHUNK, a:b], in_=result[oc][:, a:b])
 
-        for piece in range(NQ // C_PIECE):
-            make_taps(0, piece)
-        early_banks = []
-        for oc in range(EARLY_CHUNKS):
-            early_banks.append(new_banks())
-            make_dz(0, oc)
-            make_dz(1, oc)
+        STORE_CUTS = (0, 504, 1016, COLS)
+
+        banks = {}
+        dz_made = set()
+        taps_made = {}
+        done = set()
+
+        def passes():
             for s in range(SLICES):
-                multiply(0, oc, s, early_banks[oc][s])
-        for piece in range(NQ // C_PIECE):
-            make_taps(1, piece)
-        for oc in range(EARLY_CHUNKS):
-            finish(oc, early_banks[oc])
-        for oc in range(EARLY_CHUNKS, O_CHUNKS):
-            banks = new_banks()
-            make_dz(0, oc)
-            for s in range(SLICES):
-                multiply(0, oc, s, banks[s])
-            make_dz(1, oc)
-            finish(oc, banks)
+                for oc in range(O_CHUNKS):
+                    for h in range(HALVES):
+                        for g in range(G):
+                            key = (h, oc, s, g)
+                            if key in done or (h, oc) not in dz_made:
+                                continue
+                            if taps_made.get((h, g), 0) * TAPS < (s + 1) * N_TILE:
+                                continue
+                            if h == 1 and any((0, oc, s, gg) not in done for gg in range(G)):
+                                continue
+                            if h == 1 and any((1, oc, s, gg) not in done for gg in range(g)):
+                                continue
+                            if h == 0 and any((0, oc, s, gg) not in done for gg in range(g)):
+                                continue
+                            if (oc, s) not in banks:
+                                if sum(1 for b in banks if b not in emptied) >= BANKS:
+                                    continue
+                                banks[oc, s] = psum.tile([P, N_TILE], F32, name="bank")
+                            multiply(h, oc, s, g, banks[oc, s])
+                            done.add(key)
+                            if h == 1 and g == G - 1:
+                                closed.append((oc, s))
+
+        emptied = set()
+
+        def drain(count):
+            for i in range(min(count, len(closed))):
+                oc, s = closed.pop(0)
+                empty(s, banks[oc, s], result[oc], nc.vector.tensor_copy if s in V_EMPTIES else nc.scalar.copy)
+                emptied.add((oc, s))
+                if oc == O_CHUNKS - 1:
+                    store(oc, s)
+                elif s == SLICES - 1:
+                    nc.sync.dma_start(out=out_rows[oc * O_CHUNK : (oc + 1) * O_CHUNK, :], in_=result[oc][:])
+
+        def flush(keep_back):
+            while len(waiting) > keep_back:
+                key, job = waiting.pop(0)
+                job()
+                if key[0] == "Z":
+                    dz_made.add(key[1:])
+                else:
+                    taps_made[key[1], key[3]] = key[2]
+                passes()
+
+        loads = list(LOADS)
+        for i, step in enumerate(STEPS):
+            while loads and loads[0][0] <= i:
+                load(*loads.pop(0)[1])
+            kind, h = step[:2]
+            if kind == "T":
+                for g in range(G):
+                    tap_unit(h, step[2], step[3], g)
+                    drain(DRAIN)
+                    flush(1)
+            else:
+                dz_unit(h, step[2])
+                drain(DRAIN)
+                flush(1)
+        flush(0)
+        drain(O_CHUNKS * SLICES)

@@ -17,7 +17,6 @@ HALVES = N // K_PASS
 COLS = NQ * TAPS
 N_TILE = 512
 SLICES = COLS // N_TILE
-WIDE = 256
 QUAD = 4
 QUAD_COLS = QUAD * TAPS
 O_CHUNK = P
@@ -28,12 +27,15 @@ BANKS = 8
 BANK_BUFS = 8
 WIDEST_PIECE = 256
 DRAIN = 2
-V_SHARE = (512, 512, 256)
-RAW_BUFS = 6
-V_DZ = {(h, oc): 0 for h in range(2) for oc in range(4)}
-STEPS = (("T", 0, 0, 64), ("T", 0, 64, 192), ("T", 0, 256, 256), ("Z", 0, 0), ("Z", 0, 1), ("T", 1, 0, 256), ("T", 1, 256, 256), ("Z", 1, 0), ("Z", 1, 1), ("Z", 0, 2), ("Z", 0, 3), ("Z", 1, 2), ("Z", 1, 3))
-LOADS = ((0, ("T", 0, 0, 64)), (0, ("T", 0, 64, 192)), (0, ("T", 0, 256, 256)), (0, ("Z", 0, 0, 256)), (0, ("T", 1, 0, 256)), (0, ("T", 1, 256, 256)), (0, ("Z", 1, 0, 256)), (2, ("Z", 0, 256, 256)), (3, ("Z", 1, 256, 128)), (3, ("Z", 1, 384, 128)))
-V_EMPTIES = (1,)
+V_SHARE = (512, 512, 128)
+RAW_BUFS = 5
+V_DZ = {(h, oc): (64 if (h, oc) == (1, 3) else 0) for h in range(2) for oc in range(4)}
+STEPS = (("T", 0, 0, 64), ("T", 0, 64, 192), ("T", 0, 256, 256), ("Z", 0, 0), ("Z", 0, 1), ("T", 1, 0, 256), ("T", 1, 256, 256), ("Z", 1, 0), ("Z", 1, 1), ("Z", 0, 2), ("Z", 1, 2), ("Z", 0, 3), ("Z", 1, 3))
+LOADS = ((0, ("x", 0, 0, 64)), (0, ("q", 0, 0, 64)), (0, ("x", 0, 64, 192)), (0, ("q", 0, 64, 192)), (0, ("x", 0, 256, 256)), (0, ("q", 0, 256, 256)), (0, ("z", 0, 0, 256)), (0, ("g", 0, 0, 256)), (0, ("x", 1, 0, 256)), (0, ("q", 1, 0, 256)), (0, ("x", 1, 256, 256)), (0, ("q", 1, 256, 256)), (2, ("z", 1, 0, 256)), (3, ("g", 1, 0, 256)), (3, ("g", 0, 256, 256)), (3, ("z", 0, 256, 128)), (5, ("g", 1, 256, 256)), (5, ("z", 1, 256, 128)), (5, ("z", 0, 384, 128)), (5, ("z", 1, 384, 128)))
+V_EMPTIES = ((0, 1), (1, 1), (2, 1), (3, 1))
+TAIL = 2
+NARROW_BUFS = 5
+LAG = 1
 
 FLOPS = 2 * N * G * NQ * COLS
 BYTES = 2 * N * NQ * (2 * G + G + G) + 4 * N * NQ * G + 4 * NQ * COLS
@@ -58,7 +60,9 @@ def tile_quadjetresnetblock_pb_v_kernel(tc, x, q2, q1, W3, b3, z, grad_out, out)
 
     with ExitStack() as ctx:
         keep = ctx.enter_context(tc.tile_pool(name="keep", bufs=1))
-        taps_grouped = ctx.enter_context(tc.tile_pool(name="taps_grouped", bufs=3))
+        taps_grouped = ctx.enter_context(tc.tile_pool(name="taps_grouped", bufs=LAG + 2))
+        raw_narrow = ctx.enter_context(tc.tile_pool(name="raw_narrow", bufs=NARROW_BUFS))
+        raw_late = ctx.enter_context(tc.tile_pool(name="raw_late", bufs=4))
         raw = ctx.enter_context(tc.tile_pool(name="raw", bufs=RAW_BUFS))
         dz_work = ctx.enter_context(tc.tile_pool(name="dz_work", bufs=2))
         psum = ctx.enter_context(tc.psum_pool(name="psum", bufs=BANK_BUFS))
@@ -86,45 +90,44 @@ def tile_quadjetresnetblock_pb_v_kernel(tc, x, q2, q1, W3, b3, z, grad_out, out)
         tiles = {}
 
         def load(kind, h, first, width):
-            if first % WIDE == 0:
-                if kind == "T":
-                    tiles[kind, h, first // WIDE] = (
-                        raw.tile([P, PACK, WIDE, 2 * G], BF16, name="raw_wide"),
-                        raw.tile([P, PACK, WIDE, G], BF16, name="raw_narrow"),
-                    )
-                else:
-                    tiles[kind, h, first // WIDE] = (
-                        raw.tile([P, PACK, WIDE, G], F32, name="raw_wide"),
-                        raw.tile([P, PACK, WIDE, G], BF16, name="raw_narrow"),
-                    )
-            here = slice(first % WIDE, first % WIDE + width)
-            for tile, src in zip(tiles[kind, h, first // WIDE], (x, q2) if kind == "T" else (z, grad_out)):
-                nc.sync.dma_start(out=tile[:, :, here, :], in_=rows_of(src, h, first, width))
+            src, dtype, steps = {"x": (x, BF16, 2 * G), "q": (q2, BF16, G), "z": (z, F32, G), "g": (grad_out, BF16, G)}[kind]
+            if (h, first) == (0, 0) and kind in "xq":
+                tile = keep.tile([P, PACK, width, steps], dtype, name="first_" + kind)
+            elif kind == "z" and width == O_CHUNK:
+                tile = raw_late.tile([P, PACK, width, steps], dtype, name="raw_late")
+            elif kind in "xz":
+                tile = raw.tile([P, PACK, width, steps], dtype, name="raw_wide")
+            else:
+                tile = raw_narrow.tile([P, PACK, width, steps], dtype, name="raw_narrow")
+            nc.sync.dma_start(out=tile[:], in_=rows_of(src, h, first, width))
+            tiles.setdefault((kind, h), []).append((first, first + width, tile))
+
+        def loaded(kind, h, first, width):
+            for a, b, tile in tiles[kind, h]:
+                if a <= first and first + width <= b:
+                    return tile[:, :, first - a : first - a + width, :]
 
         waiting = []
         closed = []
 
         def tap_unit(h, first, width, g):
-            x_raw, q2_raw = tiles["T", h, first // WIDE]
-            lo = first % WIDE
-            chans = slice(lo, lo + width)
+            x_raw, q2_raw = loaded("x", h, first, width), loaded("q", h, first, width)
             grouped = taps_grouped.tile([P, WIDEST_PIECE // QUAD, TAPS, QUAD, PACK], BF16, align_bytes=64, name="grouped")[:, : width // QUAD]
             nc.scalar.copy(
                 out=grouped[:, :, 2, :, :].rearrange("p q c j -> p q j c"),
-                in_=q2_raw[:, :, chans, g].rearrange("p j (q c) -> p q j c", c=QUAD),
+                in_=q2_raw[:, :, :, g].rearrange("p j (q c) -> p q j c", c=QUAD),
             )
             cut = V_SHARE[g] * width // 512 // (2 * QUAD) * 2
             if cut:
                 nc.vector.tensor_copy(
                     out=grouped[:, :cut, 0:2, :, :].rearrange("p q t c j -> p q j c t"),
-                    in_=x_raw[:, :, lo : lo + cut * QUAD, 2 * g : 2 * g + 2].rearrange("p j (q c) t -> p q j c t", c=QUAD),
+                    in_=x_raw[:, :, : cut * QUAD, 2 * g : 2 * g + 2].rearrange("p j (q c) t -> p q j c t", c=QUAD),
                 )
             if cut * QUAD < width:
-                for t in range(2):
-                    nc.scalar.copy(
-                        out=grouped[:, cut:, t, :, :].rearrange("p q c j -> p q j c"),
-                        in_=x_raw[:, :, lo + cut * QUAD : lo + width, 2 * g + t].rearrange("p j (q c) -> p q j c", c=QUAD),
-                    )
+                nc.scalar.copy(
+                    out=grouped[:, cut:, 0:2, :, :].rearrange("p q t c j -> p q j c t"),
+                    in_=x_raw[:, :, cut * QUAD :, 2 * g : 2 * g + 2].rearrange("p j (q c) t -> p q j c t", c=QUAD),
+                )
             cols = slice(first * TAPS, (first + width) * TAPS)
             waiting.append((
                 ("T", h, first + width, g),
@@ -137,31 +140,34 @@ def tile_quadjetresnetblock_pb_v_kernel(tc, x, q2, q1, W3, b3, z, grad_out, out)
             ))
 
         def dz_unit(h, oc):
-            z_raw, grad_raw = tiles["Z", h, oc * O_CHUNK // WIDE]
-            first = oc * O_CHUNK % WIDE
-            part = slice(first, first + O_CHUNK)
+            z_raw, grad_raw = loaded("z", h, oc * O_CHUNK, O_CHUNK), loaded("g", h, oc * O_CHUNK, O_CHUNK)
             dz_rows = dz_work.tile([P, PACK, O_CHUNK, G], BF16, name="dz_rows")
             nc.vector.scalar_tensor_tensor(
                 out=dz_rows[:].rearrange("p j o g -> p j (o g)"),
-                in0=z_raw[:, :, part, :].rearrange("p j o g -> p j (o g)"),
+                in0=z_raw.rearrange("p j o g -> p j (o g)"),
                 scalar=0.0,
-                in1=grad_raw[:, :, part, :].rearrange("p j o g -> p j (o g)"),
+                in1=grad_raw.rearrange("p j o g -> p j (o g)"),
                 op0=mybir.AluOpType.is_gt,
                 op1=mybir.AluOpType.mult,
             )
+            if (h, oc) == (HALVES - 1, O_CHUNKS - 1):
+                flush(0)
             grouped = dz_work.tile([P, G, O_CHUNK, PACK], BF16, align_bytes=64, name="dz_grouped")
             for copy, o_range in ((nc.vector.tensor_copy, slice(0, V_DZ[h, oc])), (nc.scalar.copy, slice(V_DZ[h, oc], O_CHUNK))):
                 if o_range.start < o_range.stop:
                     copy(
-                        out=grouped[:, :, o_range, :].rearrange("p g o j -> p o j g"),
-                        in_=dz_rows[:, :, o_range, :].rearrange("p j o g -> p o j g"),
+                        out=grouped[:, :, o_range, :].rearrange("p g (q o) j -> p q j o g", o=2),
+                        in_=dz_rows[:, :, o_range, :].rearrange("p j (q o) g -> p q j o g", o=2),
                     )
-            waiting.append((
-                ("Z", h, oc),
-                lambda: quantise(
-                    grouped[:].rearrange("p g o j -> p (g o j)"), dz_codes[:, h, oc, :], dz_scales[:, h, oc, :], E5M2X4
-                ),
-            ))
+            parts = [(g, g + 1) for g in range(G)] if (h, oc) == (HALVES - 1, O_CHUNKS - 1) else [(0, G)]
+            for a, b in parts:
+                words = slice(a * O_CHUNK, b * O_CHUNK)
+                waiting.append((
+                    ("Z", h, oc, a, b),
+                    lambda a=a, b=b, words=words: quantise(
+                        grouped[:, a:b].rearrange("p g o j -> p (g o j)"), dz_codes[:, h, oc, words], dz_scales[:, h, oc, words], E5M2X4
+                    ),
+                ))
 
         def multiply(h, oc, s, g, bank):
             cols = slice(s * N_TILE, (s + 1) * N_TILE)
@@ -210,7 +216,7 @@ def tile_quadjetresnetblock_pb_v_kernel(tc, x, q2, q1, W3, b3, z, grad_out, out)
                     for h in range(HALVES):
                         for g in range(G):
                             key = (h, oc, s, g)
-                            if key in done or (h, oc) not in dz_made:
+                            if key in done or (h, oc, g) not in dz_made:
                                 continue
                             if taps_made.get((h, g), 0) * TAPS < (s + 1) * N_TILE:
                                 continue
@@ -234,7 +240,7 @@ def tile_quadjetresnetblock_pb_v_kernel(tc, x, q2, q1, W3, b3, z, grad_out, out)
         def drain(count):
             for i in range(min(count, len(closed))):
                 oc, s = closed.pop(0)
-                empty(s, banks[oc, s], result[oc], nc.vector.tensor_copy if s in V_EMPTIES else nc.scalar.copy)
+                empty(s, banks[oc, s], result[oc], nc.vector.tensor_copy if (oc, s) in V_EMPTIES else nc.scalar.copy)
                 emptied.add((oc, s))
                 if oc == O_CHUNKS - 1:
                     store(oc, s)
@@ -246,7 +252,8 @@ def tile_quadjetresnetblock_pb_v_kernel(tc, x, q2, q1, W3, b3, z, grad_out, out)
                 key, job = waiting.pop(0)
                 job()
                 if key[0] == "Z":
-                    dz_made.add(key[1:])
+                    for g in range(key[3], key[4]):
+                        dz_made.add((key[1], key[2], g))
                 else:
                     taps_made[key[1], key[3]] = key[2]
                 passes()
@@ -256,14 +263,18 @@ def tile_quadjetresnetblock_pb_v_kernel(tc, x, q2, q1, W3, b3, z, grad_out, out)
             while loads and loads[0][0] <= i:
                 load(*loads.pop(0)[1])
             kind, h = step[:2]
+            late = i >= len(STEPS) - TAIL
             if kind == "T":
                 for g in range(G):
                     tap_unit(h, step[2], step[3], g)
                     drain(DRAIN)
-                    flush(1)
+                    flush(LAG)
             else:
                 dz_unit(h, step[2])
-                drain(DRAIN)
+                if not late:
+                    drain(DRAIN)
                 flush(1)
+                if late:
+                    drain(DRAIN)
         flush(0)
         drain(O_CHUNKS * SLICES)

@@ -27,15 +27,15 @@ BANKS = 8
 BANK_BUFS = 8
 WIDEST_PIECE = 256
 DRAIN = 2
-V_SHARE = (512, 512, 128)
 RAW_BUFS = 5
-V_DZ = {(h, oc): (64 if (h, oc) == (1, 3) else 0) for h in range(2) for oc in range(4)}
 STEPS = (("T", 0, 0, 64), ("T", 0, 64, 192), ("T", 0, 256, 256), ("Z", 0, 0), ("Z", 0, 1), ("T", 1, 0, 256), ("T", 1, 256, 256), ("Z", 1, 0), ("Z", 1, 1), ("Z", 0, 2), ("Z", 1, 2), ("Z", 0, 3), ("Z", 1, 3))
-LOADS = ((0, ("x", 0, 0, 64)), (0, ("q", 0, 0, 64)), (0, ("x", 0, 64, 192)), (0, ("q", 0, 64, 192)), (0, ("x", 0, 256, 256)), (0, ("q", 0, 256, 256)), (0, ("z", 0, 0, 256)), (0, ("g", 0, 0, 256)), (0, ("x", 1, 0, 256)), (0, ("q", 1, 0, 256)), (0, ("x", 1, 256, 256)), (0, ("q", 1, 256, 256)), (2, ("z", 1, 0, 256)), (3, ("g", 1, 0, 256)), (3, ("g", 0, 256, 256)), (3, ("z", 0, 256, 128)), (5, ("g", 1, 256, 256)), (5, ("z", 1, 256, 128)), (5, ("z", 0, 384, 128)), (5, ("z", 1, 384, 128)))
+LOADS = ((0, ("x", 0, 0, 64)), (0, ("q", 0, 0, 64)), (0, ("x", 0, 64, 192)), (0, ("q", 0, 64, 192)), (0, ("x", 0, 256, 256)), (0, ("q", 0, 256, 256)), (0, ("z", 0, 0, 256)), (0, ("g", 0, 0, 256)), (0, ("x", 1, 0, 256)), (0, ("q", 1, 0, 256)), (0, ("x", 1, 256, 256)), (0, ("q", 1, 256, 256)), (2, ("z", 1, 0, 256)), (3, ("g", 1, 0, 256)), (3, ("g", 0, 256, 256)), (3, ("z", 0, 256, 128)), (5, ("g", 1, 256, 256)), (5, ("z", 1, 256, 128)), (5, ("z", 0, 384, 128)), (10, ("z", 1, 384, 128)))
 V_EMPTIES = ((0, 1), (1, 1), (2, 1), (3, 1))
-TAIL = 2
+TAIL = 1
 NARROW_BUFS = 5
 LAG = 1
+LAST_CUTS = ((0, 128, 40),)
+X_ON_SCALAR = ((1, 256, 2),)
 
 FLOPS = 2 * N * G * NQ * COLS
 BYTES = 2 * N * NQ * (2 * G + G + G) + 4 * N * NQ * G + 4 * NQ * COLS
@@ -62,7 +62,7 @@ def tile_quadjetresnetblock_pb_v_kernel(tc, x, q2, q1, W3, b3, z, grad_out, out)
         keep = ctx.enter_context(tc.tile_pool(name="keep", bufs=1))
         taps_grouped = ctx.enter_context(tc.tile_pool(name="taps_grouped", bufs=LAG + 2))
         raw_narrow = ctx.enter_context(tc.tile_pool(name="raw_narrow", bufs=NARROW_BUFS))
-        raw_late = ctx.enter_context(tc.tile_pool(name="raw_late", bufs=4))
+        raw_late = ctx.enter_context(tc.tile_pool(name="raw_late", bufs=3))
         raw = ctx.enter_context(tc.tile_pool(name="raw", bufs=RAW_BUFS))
         dz_work = ctx.enter_context(tc.tile_pool(name="dz_work", bufs=2))
         psum = ctx.enter_context(tc.psum_pool(name="psum", bufs=BANK_BUFS))
@@ -117,7 +117,7 @@ def tile_quadjetresnetblock_pb_v_kernel(tc, x, q2, q1, W3, b3, z, grad_out, out)
                 out=grouped[:, :, 2, :, :].rearrange("p q c j -> p q j c"),
                 in_=q2_raw[:, :, :, g].rearrange("p j (q c) -> p q j c", c=QUAD),
             )
-            cut = V_SHARE[g] * width // 512 // (2 * QUAD) * 2
+            cut = 0 if (h, first, g) in X_ON_SCALAR else width // QUAD
             if cut:
                 nc.vector.tensor_copy(
                     out=grouped[:, :cut, 0:2, :, :].rearrange("p q t c j -> p q j c t"),
@@ -142,24 +142,27 @@ def tile_quadjetresnetblock_pb_v_kernel(tc, x, q2, q1, W3, b3, z, grad_out, out)
         def dz_unit(h, oc):
             z_raw, grad_raw = loaded("z", h, oc * O_CHUNK, O_CHUNK), loaded("g", h, oc * O_CHUNK, O_CHUNK)
             dz_rows = dz_work.tile([P, PACK, O_CHUNK, G], BF16, name="dz_rows")
-            nc.vector.scalar_tensor_tensor(
-                out=dz_rows[:].rearrange("p j o g -> p j (o g)"),
-                in0=z_raw.rearrange("p j o g -> p j (o g)"),
-                scalar=0.0,
-                in1=grad_raw.rearrange("p j o g -> p j (o g)"),
-                op0=mybir.AluOpType.is_gt,
-                op1=mybir.AluOpType.mult,
-            )
-            if (h, oc) == (HALVES - 1, O_CHUNKS - 1):
-                flush(0)
             grouped = dz_work.tile([P, G, O_CHUNK, PACK], BF16, align_bytes=64, name="dz_grouped")
-            for copy, o_range in ((nc.vector.tensor_copy, slice(0, V_DZ[h, oc])), (nc.scalar.copy, slice(V_DZ[h, oc], O_CHUNK))):
-                if o_range.start < o_range.stop:
-                    copy(
-                        out=grouped[:, :, o_range, :].rearrange("p g (q o) j -> p q j o g", o=2),
-                        in_=dz_rows[:, :, o_range, :].rearrange("p j (q o) g -> p q j o g", o=2),
-                    )
-            parts = [(g, g + 1) for g in range(G)] if (h, oc) == (HALVES - 1, O_CHUNKS - 1) else [(0, G)]
+            last = (h, oc) == (HALVES - 1, O_CHUNKS - 1)
+            cuts = LAST_CUTS if last else ((0, O_CHUNK, 0),)
+            for a, b, to_vector in cuts:
+                nc.vector.scalar_tensor_tensor(
+                    out=dz_rows[:, :, a:b, :].rearrange("p j o g -> p j (o g)"),
+                    in0=z_raw[:, :, a:b, :].rearrange("p j o g -> p j (o g)"),
+                    scalar=0.0,
+                    in1=grad_raw[:, :, a:b, :].rearrange("p j o g -> p j (o g)"),
+                    op0=mybir.AluOpType.is_gt,
+                    op1=mybir.AluOpType.mult,
+                )
+                if last and b == O_CHUNK:
+                    flush(0)
+                for copy, c, d in ((nc.scalar.copy, a, b - to_vector), (nc.vector.tensor_copy, b - to_vector, b)):
+                    if c < d:
+                        copy(
+                            out=grouped[:, :, c:d, :].rearrange("p g (q o) j -> p q j o g", o=2),
+                            in_=dz_rows[:, :, c:d, :].rearrange("p j (q o) g -> p q j o g", o=2),
+                        )
+            parts = [(0, G)]
             for a, b in parts:
                 words = slice(a * O_CHUNK, b * O_CHUNK)
                 waiting.append((
@@ -182,17 +185,21 @@ def tile_quadjetresnetblock_pb_v_kernel(tc, x, q2, q1, W3, b3, z, grad_out, out)
                 stop=(h == HALVES - 1 and g == G - 1),
             )
 
-        def empty(s, bank, result, copy):
+        def empty(s, bank, result, copies):
             lo, hi = s * N_TILE, (s + 1) * N_TILE
             first_quad, last_quad = -(-lo // QUAD_COLS), hi // QUAD_COLS
-            copy(
-                out=result[:, first_quad * QUAD_COLS : last_quad * QUAD_COLS].rearrange("p (q c t) -> p q c t", t=TAPS, c=QUAD),
-                in_=bank[:, first_quad * QUAD_COLS - lo : last_quad * QUAD_COLS - lo].rearrange("p (q t c) -> p q c t", t=TAPS, c=QUAD),
-            )
+            n = len(copies)
+            for i, copy in enumerate(copies):
+                a = first_quad + (last_quad - first_quad) * i // n
+                b = first_quad + (last_quad - first_quad) * (i + 1) // n
+                copy(
+                    out=result[:, a * QUAD_COLS : b * QUAD_COLS].rearrange("p (q c t) -> p q c t", t=TAPS, c=QUAD),
+                    in_=bank[:, a * QUAD_COLS - lo : b * QUAD_COLS - lo].rearrange("p (q t c) -> p q c t", t=TAPS, c=QUAD),
+                )
             for quad, a, b in ((first_quad - 1, lo, first_quad * QUAD_COLS), (last_quad, last_quad * QUAD_COLS, hi)):
                 if a < b:
                     start = quad * QUAD_COLS
-                    copy(
+                    copies[-1](
                         out=result[:, start : start + QUAD_COLS].rearrange("p (c t) -> p c t", t=TAPS)[
                             :, :, (a - start) // QUAD : (b - start) // QUAD
                         ],
@@ -240,7 +247,7 @@ def tile_quadjetresnetblock_pb_v_kernel(tc, x, q2, q1, W3, b3, z, grad_out, out)
         def drain(count):
             for i in range(min(count, len(closed))):
                 oc, s = closed.pop(0)
-                empty(s, banks[oc, s], result[oc], nc.vector.tensor_copy if (oc, s) in V_EMPTIES else nc.scalar.copy)
+                empty(s, banks[oc, s], result[oc], [nc.scalar.copy, nc.vector.tensor_copy] if (oc, s) == (O_CHUNKS - 1, SLICES - 1) else [nc.vector.tensor_copy if (oc, s) in V_EMPTIES else nc.scalar.copy])
                 emptied.add((oc, s))
                 if oc == O_CHUNKS - 1:
                     store(oc, s)

@@ -27,15 +27,16 @@ BANKS = 8
 BANK_BUFS = 8
 WIDEST_PIECE = 256
 DRAIN = 2
-RAW_BUFS = 5
+RAW_BUFS = 4
 STEPS = (("T", 0, 0, 64), ("T", 0, 64, 192), ("T", 0, 256, 256), ("Z", 0, 0), ("Z", 0, 1), ("T", 1, 0, 256), ("T", 1, 256, 256), ("Z", 1, 0), ("Z", 1, 1), ("Z", 0, 2), ("Z", 1, 2), ("Z", 0, 3), ("Z", 1, 3))
-LOADS = ((0, ("x", 0, 0, 64)), (0, ("q", 0, 0, 64)), (0, ("x", 0, 64, 192)), (0, ("q", 0, 64, 192)), (0, ("x", 0, 256, 256)), (0, ("q", 0, 256, 256)), (0, ("z", 0, 0, 256)), (0, ("g", 0, 0, 256)), (0, ("x", 1, 0, 256)), (0, ("q", 1, 0, 256)), (0, ("x", 1, 256, 256)), (0, ("q", 1, 256, 256)), (2, ("z", 1, 0, 256)), (3, ("g", 1, 0, 256)), (3, ("g", 0, 256, 256)), (3, ("z", 0, 256, 128)), (5, ("g", 1, 256, 256)), (5, ("z", 1, 256, 128)), (5, ("z", 0, 384, 128)), (10, ("z", 1, 384, 128)))
-V_EMPTIES = ((0, 1), (1, 1), (2, 1), (3, 1))
-TAIL = 1
+LOADS = ((0, ("x", 0, 0, 64)), (0, ("q", 0, 0, 64)), (0, ("x", 0, 64, 192)), (0, ("q", 0, 64, 192)), (0, ("x", 0, 256, 256)), (0, ("q", 0, 256, 256)), (0, ("g", 0, 0, 256)), (0, ("z", 0, 0, 128)), (0, ("z", 0, 128, 128)), (0, ("x", 1, 0, 256)), (0, ("q", 1, 0, 256)), (1, ("x", 1, 256, 256)), (2, ("q", 1, 256, 256)), (2, ("g", 1, 0, 256)), (2, ("z", 1, 0, 128)), (2, ("z", 1, 128, 128)), (3, ("g", 0, 256, 128)), (4, ("z", 0, 256, 128)), (5, ("g", 1, 256, 256)), (5, ("z", 1, 256, 128)), (6, ("g", 0, 384, 128)), (6, ("z", 0, 384, 128)), (8, ("z", 1, 384, 128)))
+V_EMPTIES = ((0, 1), (1, 2), (2, 1), (3, 1))
+TAIL = 4
 NARROW_BUFS = 5
 LAG = 1
 LAST_CUTS = ((0, 128, 40),)
 X_ON_SCALAR = ((1, 256, 2),)
+PE_UNITS = ()
 
 FLOPS = 2 * N * G * NQ * COLS
 BYTES = 2 * N * NQ * (2 * G + G + G) + 4 * N * NQ * G + 4 * NQ * COLS
@@ -62,7 +63,7 @@ def tile_quadjetresnetblock_pb_v_kernel(tc, x, q2, q1, W3, b3, z, grad_out, out)
         keep = ctx.enter_context(tc.tile_pool(name="keep", bufs=1))
         taps_grouped = ctx.enter_context(tc.tile_pool(name="taps_grouped", bufs=LAG + 2))
         raw_narrow = ctx.enter_context(tc.tile_pool(name="raw_narrow", bufs=NARROW_BUFS))
-        raw_late = ctx.enter_context(tc.tile_pool(name="raw_late", bufs=3))
+        raw_late = ctx.enter_context(tc.tile_pool(name="raw_late", bufs=6))
         raw = ctx.enter_context(tc.tile_pool(name="raw", bufs=RAW_BUFS))
         dz_work = ctx.enter_context(tc.tile_pool(name="dz_work", bufs=2))
         psum = ctx.enter_context(tc.psum_pool(name="psum", bufs=BANK_BUFS))

@@ -1,6 +1,7 @@
 from contextlib import ExitStack
 
 import concourse.mybir as mybir
+from concourse.masks import make_identity
 
 BF16 = mybir.dt.bfloat16
 F32 = mybir.dt.float32
@@ -29,14 +30,14 @@ WIDEST_PIECE = 256
 DRAIN = 2
 RAW_BUFS = 4
 STEPS = (("T", 0, 0, 64), ("T", 0, 64, 192), ("T", 0, 256, 256), ("Z", 0, 0), ("Z", 0, 1), ("T", 1, 0, 256), ("T", 1, 256, 256), ("Z", 1, 0), ("Z", 1, 1), ("Z", 0, 2), ("Z", 1, 2), ("Z", 0, 3), ("Z", 1, 3))
-LOADS = ((0, ("x", 0, 0, 64)), (0, ("q", 0, 0, 64)), (0, ("x", 0, 64, 192)), (0, ("q", 0, 64, 192)), (0, ("x", 0, 256, 256)), (0, ("q", 0, 256, 256)), (0, ("g", 0, 0, 256)), (0, ("z", 0, 0, 128)), (0, ("z", 0, 128, 128)), (0, ("x", 1, 0, 256)), (0, ("q", 1, 0, 256)), (1, ("x", 1, 256, 256)), (2, ("q", 1, 256, 256)), (2, ("g", 1, 0, 256)), (2, ("z", 1, 0, 128)), (2, ("z", 1, 128, 128)), (3, ("g", 0, 256, 128)), (4, ("z", 0, 256, 128)), (5, ("g", 1, 256, 256)), (5, ("z", 1, 256, 128)), (6, ("g", 0, 384, 128)), (6, ("z", 0, 384, 128)), (8, ("z", 1, 384, 128)))
+LOADS = ((0, ("x", 0, 0, 64)), (0, ("q", 0, 0, 64)), (0, ("x", 0, 64, 192)), (0, ("q", 0, 64, 192)), (0, ("x", 0, 256, 256)), (0, ("q", 0, 256, 256)), (0, ("g", 0, 0, 256)), (0, ("z", 0, 0, 128)), (0, ("z", 0, 128, 128)), (0, ("x", 1, 0, 256)), (0, ("q", 1, 0, 256)), (1, ("x", 1, 256, 256)), (2, ("q", 1, 256, 256)), (2, ("g", 1, 0, 256)), (2, ("z", 1, 0, 128)), (2, ("z", 1, 128, 128)), (3, ("g", 0, 256, 128)), (4, ("z", 0, 256, 128)), (5, ("g", 1, 256, 128)), (5, ("z", 1, 256, 128)), (6, ("g", 0, 384, 128)), (6, ("z", 0, 384, 128)), (7, ("g", 1, 384, 128)), (8, ("z", 1, 384, 128)))
 V_EMPTIES = ((0, 1), (1, 2), (2, 1), (3, 1))
 TAIL = 4
 NARROW_BUFS = 5
 LAG = 1
 LAST_CUTS = ((0, 128, 40),)
-X_ON_SCALAR = ((1, 256, 2),)
-PE_UNITS = ()
+X_ON_SCALAR = ()
+PE_UNITS = ((0, 64, 2), (0, 256, 2), (1, 256, 2))
 
 FLOPS = 2 * N * G * NQ * COLS
 BYTES = 2 * N * NQ * (2 * G + G + G) + 4 * N * NQ * G + 4 * NQ * COLS
@@ -75,6 +76,9 @@ def tile_quadjetresnetblock_pb_v_kernel(tc, x, q2, q1, W3, b3, z, grad_out, out)
         dz_scales = keep.tile([P, HALVES, O_CHUNKS, G * O_CHUNK], U8, align_bytes=64)
         result = [keep.tile([P, COLS], F32, name="result%d" % oc) for oc in range(O_CHUNKS)]
 
+        ident = keep.tile([P, P], BF16)
+        make_identity(nc, ident[:])
+
         def rows_of(src, h, first, width):
             n_rows = slice(h * K_PASS, (h + 1) * K_PASS)
             return src[n_rows, first : first + width, :].rearrange("(p j) c s -> p j c s", j=PACK)
@@ -111,6 +115,23 @@ def tile_quadjetresnetblock_pb_v_kernel(tc, x, q2, q1, W3, b3, z, grad_out, out)
         waiting = []
         closed = []
 
+        swaps = {}
+
+        def swap_x(h, first, width, g):
+            swaps[h, first, g] = []
+            for t in range(2):
+                swap = psum.tile([P, 2 * N_TILE], BF16, name="bank")
+                for a in range(0, width, P):
+                    b = min(a + P, width)
+                    nc.tensor.matmul(
+                        out=swap[:, a * PACK : b * PACK],
+                        lhsT=ident[:],
+                        rhs=loaded("x", h, first, width)[:, :, a:b, 2 * g + t].rearrange("p j c -> p c j"),
+                        start=True,
+                        stop=True,
+                    )
+                swaps[h, first, g].append(swap)
+
         def tap_unit(h, first, width, g):
             x_raw, q2_raw = loaded("x", h, first, width), loaded("q", h, first, width)
             grouped = taps_grouped.tile([P, WIDEST_PIECE // QUAD, TAPS, QUAD, PACK], BF16, align_bytes=64, name="grouped")[:, : width // QUAD]
@@ -118,16 +139,16 @@ def tile_quadjetresnetblock_pb_v_kernel(tc, x, q2, q1, W3, b3, z, grad_out, out)
                 out=grouped[:, :, 2, :, :].rearrange("p q c j -> p q j c"),
                 in_=q2_raw[:, :, :, g].rearrange("p j (q c) -> p q j c", c=QUAD),
             )
-            cut = 0 if (h, first, g) in X_ON_SCALAR else width // QUAD
-            if cut:
-                nc.vector.tensor_copy(
-                    out=grouped[:, :cut, 0:2, :, :].rearrange("p q t c j -> p q j c t"),
-                    in_=x_raw[:, :, : cut * QUAD, 2 * g : 2 * g + 2].rearrange("p j (q c) t -> p q j c t", c=QUAD),
-                )
-            if cut * QUAD < width:
-                nc.scalar.copy(
-                    out=grouped[:, cut:, 0:2, :, :].rearrange("p q t c j -> p q j c t"),
-                    in_=x_raw[:, :, cut * QUAD :, 2 * g : 2 * g + 2].rearrange("p j (q c) t -> p q j c t", c=QUAD),
+            if (h, first, g) in swaps:
+                for t, swap in enumerate(swaps.pop((h, first, g))):
+                    nc.scalar.copy(
+                        out=grouped[:, :, t, :, :].rearrange("p q c j -> p q (c j)"),
+                        in_=swap[:, : width * PACK].rearrange("p (q i) -> p q i", i=QUAD * PACK),
+                    )
+            else:
+                (nc.scalar.copy if (h, first, g) in X_ON_SCALAR else nc.vector.tensor_copy)(
+                    out=grouped[:, :, 0:2, :, :].rearrange("p q t c j -> p q j c t"),
+                    in_=x_raw[:, :, :, 2 * g : 2 * g + 2].rearrange("p j (q c) t -> p q j c t", c=QUAD),
                 )
             cols = slice(first * TAPS, (first + width) * TAPS)
             waiting.append((
@@ -274,6 +295,8 @@ def tile_quadjetresnetblock_pb_v_kernel(tc, x, q2, q1, W3, b3, z, grad_out, out)
             late = i >= len(STEPS) - TAIL
             if kind == "T":
                 for g in range(G):
+                    if (h, step[2], g) in PE_UNITS:
+                        swap_x(h, step[2], step[3], g)
                     tap_unit(h, step[2], step[3], g)
                     drain(DRAIN)
                     flush(LAG)

from contextlib import ExitStack

import concourse.mybir as mybir
from concourse.masks import make_identity

BF16 = mybir.dt.bfloat16
F32 = mybir.dt.float32
U32 = mybir.dt.uint32
U8 = mybir.dt.uint8
E4M3X4 = mybir.dt.float8_e4m3fn_x4
E5M2X4 = mybir.dt.float8_e5m2_x4

P = 128
PACK = 4
K_PASS = P * PACK
N, NQ, G, TAPS = 1024, 512, 3, 3
HALVES = N // K_PASS
COLS = NQ * TAPS
N_TILE = 512
SLICES = COLS // N_TILE
QUAD = 4
QUAD_COLS = QUAD * TAPS
O_CHUNK = P
O_CHUNKS = NQ // O_CHUNK
WIDEST_QUANTISE = 2048

BANKS = 8
BANK_BUFS = 8
WIDEST_PIECE = 256
DRAIN = 2
RAW_BUFS = 4
STEPS = (("T", 0, 0, 64), ("T", 0, 64, 192), ("T", 0, 256, 256), ("Z", 0, 0), ("Z", 0, 1), ("T", 1, 0, 256), ("T", 1, 256, 256), ("Z", 1, 0), ("Z", 1, 1), ("Z", 0, 2), ("Z", 1, 2), ("Z", 0, 3), ("Z", 1, 3))
LOADS = ((0, ("x", 0, 0, 64)), (0, ("q", 0, 0, 64)), (0, ("x", 0, 64, 192)), (0, ("q", 0, 64, 192)), (0, ("x", 0, 256, 256)), (0, ("q", 0, 256, 256)), (0, ("g", 0, 0, 256)), (0, ("z", 0, 0, 128)), (0, ("z", 0, 128, 128)), (0, ("x", 1, 0, 256)), (0, ("q", 1, 0, 256)), (1, ("x", 1, 256, 256)), (2, ("q", 1, 256, 256)), (2, ("g", 1, 0, 256)), (2, ("z", 1, 0, 128)), (2, ("z", 1, 128, 128)), (3, ("g", 0, 256, 128)), (4, ("z", 0, 256, 128)), (5, ("g", 1, 256, 128)), (5, ("z", 1, 256, 128)), (6, ("g", 0, 384, 128)), (6, ("z", 0, 384, 128)), (7, ("g", 1, 384, 128)), (8, ("z", 1, 384, 128)))
V_EMPTIES = ((0, 1), (1, 2), (2, 1), (3, 1))
TAIL = 4
NARROW_BUFS = 5
LAG = 1
LAST_CUTS = ((0, 128, 40),)
X_ON_SCALAR = ()
PE_UNITS = ((0, 64, 2), (0, 256, 2), (1, 256, 2))

FLOPS = 2 * N * G * NQ * COLS
BYTES = 2 * N * NQ * (2 * G + G + G) + 4 * N * NQ * G + 4 * NQ * COLS


def power_of_two_cuts(total):
    cuts = []
    start = 0
    width = WIDEST_QUANTISE
    while start < total:
        if width <= total - start:
            cuts.append((start, width))
            start += width
        else:
            width //= 2
    return cuts


def tile_quadjetresnetblock_pb_v_kernel(tc, x, q2, q1, W3, b3, z, grad_out, out):
    nc = tc.nc
    out_rows = out.rearrange("o c t -> o (c t)")

    with ExitStack() as ctx:
        keep = ctx.enter_context(tc.tile_pool(name="keep", bufs=1))
        taps_grouped = ctx.enter_context(tc.tile_pool(name="taps_grouped", bufs=LAG + 2))
        raw_narrow = ctx.enter_context(tc.tile_pool(name="raw_narrow", bufs=NARROW_BUFS))
        raw_late = ctx.enter_context(tc.tile_pool(name="raw_late", bufs=6))
        raw = ctx.enter_context(tc.tile_pool(name="raw", bufs=RAW_BUFS))
        dz_work = ctx.enter_context(tc.tile_pool(name="dz_work", bufs=2))
        psum = ctx.enter_context(tc.psum_pool(name="psum", bufs=BANK_BUFS))
        ctx.enter_context(tc.manual_schedule())

        tap_codes = keep.tile([P, HALVES, G, COLS], U32, align_bytes=64)
        tap_scales = keep.tile([P, HALVES, G, COLS], U8, align_bytes=64)
        dz_codes = keep.tile([P, HALVES, O_CHUNKS, G * O_CHUNK], U32, align_bytes=64)
        dz_scales = keep.tile([P, HALVES, O_CHUNKS, G * O_CHUNK], U8, align_bytes=64)
        result = [keep.tile([P, COLS], F32, name="result%d" % oc) for oc in range(O_CHUNKS)]

        ident = keep.tile([P, P], BF16)
        make_identity(nc, ident[:])

        def rows_of(src, h, first, width):
            n_rows = slice(h * K_PASS, (h + 1) * K_PASS)
            return src[n_rows, first : first + width, :].rearrange("(p j) c s -> p j c s", j=PACK)

        def quantise(grouped_flat, codes, scales, x4):
            for start, width in power_of_two_cuts(grouped_flat.shape[1]):
                words = slice(start // PACK, (start + width) // PACK)
                nc.vector.quantize_mx(
                    out=codes[:, words].bitcast(x4),
                    scales=scales[:, words],
                    in_=grouped_flat[:, start : start + width],
                )

        tiles = {}

        def load(kind, h, first, width):
            src, dtype, steps = {"x": (x, BF16, 2 * G), "q": (q2, BF16, G), "z": (z, F32, G), "g": (grad_out, BF16, G)}[kind]
            if (h, first) == (0, 0) and kind in "xq":
                tile = keep.tile([P, PACK, width, steps], dtype, name="first_" + kind)
            elif kind == "z" and width == O_CHUNK:
                tile = raw_late.tile([P, PACK, width, steps], dtype, name="raw_late")
            elif kind in "xz":
                tile = raw.tile([P, PACK, width, steps], dtype, name="raw_wide")
            else:
                tile = raw_narrow.tile([P, PACK, width, steps], dtype, name="raw_narrow")
            nc.sync.dma_start(out=tile[:], in_=rows_of(src, h, first, width))
            tiles.setdefault((kind, h), []).append((first, first + width, tile))

        def loaded(kind, h, first, width):
            for a, b, tile in tiles[kind, h]:
                if a <= first and first + width <= b:
                    return tile[:, :, first - a : first - a + width, :]

        waiting = []
        closed = []

        swaps = {}

        def swap_x(h, first, width, g):
            swaps[h, first, g] = []
            for t in range(2):
                swap = psum.tile([P, 2 * N_TILE], BF16, name="bank")
                for a in range(0, width, P):
                    b = min(a + P, width)
                    nc.tensor.matmul(
                        out=swap[:, a * PACK : b * PACK],
                        lhsT=ident[:],
                        rhs=loaded("x", h, first, width)[:, :, a:b, 2 * g + t].rearrange("p j c -> p c j"),
                        start=True,
                        stop=True,
                    )
                swaps[h, first, g].append(swap)

        def tap_unit(h, first, width, g):
            x_raw, q2_raw = loaded("x", h, first, width), loaded("q", h, first, width)
            grouped = taps_grouped.tile([P, WIDEST_PIECE // QUAD, TAPS, QUAD, PACK], BF16, align_bytes=64, name="grouped")[:, : width // QUAD]
            nc.scalar.copy(
                out=grouped[:, :, 2, :, :].rearrange("p q c j -> p q j c"),
                in_=q2_raw[:, :, :, g].rearrange("p j (q c) -> p q j c", c=QUAD),
            )
            if (h, first, g) in swaps:
                for t, swap in enumerate(swaps.pop((h, first, g))):
                    nc.scalar.copy(
                        out=grouped[:, :, t, :, :].rearrange("p q c j -> p q (c j)"),
                        in_=swap[:, : width * PACK].rearrange("p (q i) -> p q i", i=QUAD * PACK),
                    )
            else:
                (nc.scalar.copy if (h, first, g) in X_ON_SCALAR else nc.vector.tensor_copy)(
                    out=grouped[:, :, 0:2, :, :].rearrange("p q t c j -> p q j c t"),
                    in_=x_raw[:, :, :, 2 * g : 2 * g + 2].rearrange("p j (q c) t -> p q j c t", c=QUAD),
                )
            cols = slice(first * TAPS, (first + width) * TAPS)
            waiting.append((
                ("T", h, first + width, g),
                lambda: quantise(
                    grouped.rearrange("p q t c j -> p (q t c j)"),
                    tap_codes[:, h, g, cols],
                    tap_scales[:, h, g, cols],
                    E4M3X4,
                ),
            ))

        def dz_unit(h, oc):
            z_raw, grad_raw = loaded("z", h, oc * O_CHUNK, O_CHUNK), loaded("g", h, oc * O_CHUNK, O_CHUNK)
            dz_rows = dz_work.tile([P, PACK, O_CHUNK, G], BF16, name="dz_rows")
            grouped = dz_work.tile([P, G, O_CHUNK, PACK], BF16, align_bytes=64, name="dz_grouped")
            last = (h, oc) == (HALVES - 1, O_CHUNKS - 1)
            cuts = LAST_CUTS if last else ((0, O_CHUNK, 0),)
            for a, b, to_vector in cuts:
                nc.vector.scalar_tensor_tensor(
                    out=dz_rows[:, :, a:b, :].rearrange("p j o g -> p j (o g)"),
                    in0=z_raw[:, :, a:b, :].rearrange("p j o g -> p j (o g)"),
                    scalar=0.0,
                    in1=grad_raw[:, :, a:b, :].rearrange("p j o g -> p j (o g)"),
                    op0=mybir.AluOpType.is_gt,
                    op1=mybir.AluOpType.mult,
                )
                if last and b == O_CHUNK:
                    flush(0)
                for copy, c, d in ((nc.scalar.copy, a, b - to_vector), (nc.vector.tensor_copy, b - to_vector, b)):
                    if c < d:
                        copy(
                            out=grouped[:, :, c:d, :].rearrange("p g (q o) j -> p q j o g", o=2),
                            in_=dz_rows[:, :, c:d, :].rearrange("p j (q o) g -> p q j o g", o=2),
                        )
            parts = [(0, G)]
            for a, b in parts:
                words = slice(a * O_CHUNK, b * O_CHUNK)
                waiting.append((
                    ("Z", h, oc, a, b),
                    lambda a=a, b=b, words=words: quantise(
                        grouped[:, a:b].rearrange("p g o j -> p (g o j)"), dz_codes[:, h, oc, words], dz_scales[:, h, oc, words], E5M2X4
                    ),
                ))

        def multiply(h, oc, s, g, bank):
            cols = slice(s * N_TILE, (s + 1) * N_TILE)
            o_words = slice(g * O_CHUNK, (g + 1) * O_CHUNK)
            nc.tensor.matmul_mx(
                out=bank[:],
                lhsT=dz_codes[:, h, oc, o_words].bitcast(E5M2X4),
                lhsT_scale=dz_scales[:, h, oc, o_words],
                rhs=tap_codes[:, h, g, cols].bitcast(E4M3X4),
                rhs_scale=tap_scales[:, h, g, cols],
                start=(h == 0 and g == 0),
                stop=(h == HALVES - 1 and g == G - 1),
            )

        def empty(s, bank, result, copies):
            lo, hi = s * N_TILE, (s + 1) * N_TILE
            first_quad, last_quad = -(-lo // QUAD_COLS), hi // QUAD_COLS
            n = len(copies)
            for i, copy in enumerate(copies):
                a = first_quad + (last_quad - first_quad) * i // n
                b = first_quad + (last_quad - first_quad) * (i + 1) // n
                copy(
                    out=result[:, a * QUAD_COLS : b * QUAD_COLS].rearrange("p (q c t) -> p q c t", t=TAPS, c=QUAD),
                    in_=bank[:, a * QUAD_COLS - lo : b * QUAD_COLS - lo].rearrange("p (q t c) -> p q c t", t=TAPS, c=QUAD),
                )
            for quad, a, b in ((first_quad - 1, lo, first_quad * QUAD_COLS), (last_quad, last_quad * QUAD_COLS, hi)):
                if a < b:
                    start = quad * QUAD_COLS
                    copies[-1](
                        out=result[:, start : start + QUAD_COLS].rearrange("p (c t) -> p c t", t=TAPS)[
                            :, :, (a - start) // QUAD : (b - start) // QUAD
                        ],
                        in_=bank[:, a - lo : b - lo].rearrange("p (t c) -> p c t", c=QUAD),
                    )

        def store(oc, s):
            a, b = STORE_CUTS[s], STORE_CUTS[s + 1]
            nc.sync.dma_start(out=out_rows[oc * O_CHUNK : (oc + 1) * O_CHUNK, a:b], in_=result[oc][:, a:b])

        STORE_CUTS = (0, 504, 1016, COLS)

        banks = {}
        dz_made = set()
        taps_made = {}
        done = set()

        def passes():
            for s in range(SLICES):
                for oc in range(O_CHUNKS):
                    for h in range(HALVES):
                        for g in range(G):
                            key = (h, oc, s, g)
                            if key in done or (h, oc, g) not in dz_made:
                                continue
                            if taps_made.get((h, g), 0) * TAPS < (s + 1) * N_TILE:
                                continue
                            if h == 1 and any((0, oc, s, gg) not in done for gg in range(G)):
                                continue
                            if h == 1 and any((1, oc, s, gg) not in done for gg in range(g)):
                                continue
                            if h == 0 and any((0, oc, s, gg) not in done for gg in range(g)):
                                continue
                            if (oc, s) not in banks:
                                if sum(1 for b in banks if b not in emptied) >= BANKS:
                                    continue
                                banks[oc, s] = psum.tile([P, N_TILE], F32, name="bank")
                            multiply(h, oc, s, g, banks[oc, s])
                            done.add(key)
                            if h == 1 and g == G - 1:
                                closed.append((oc, s))

        emptied = set()

        def drain(count):
            for i in range(min(count, len(closed))):
                oc, s = closed.pop(0)
                empty(s, banks[oc, s], result[oc], [nc.scalar.copy, nc.vector.tensor_copy] if (oc, s) == (O_CHUNKS - 1, SLICES - 1) else [nc.vector.tensor_copy if (oc, s) in V_EMPTIES else nc.scalar.copy])
                emptied.add((oc, s))
                if oc == O_CHUNKS - 1:
                    store(oc, s)
                elif s == SLICES - 1:
                    nc.sync.dma_start(out=out_rows[oc * O_CHUNK : (oc + 1) * O_CHUNK, :], in_=result[oc][:])

        def flush(keep_back):
            while len(waiting) > keep_back:
                key, job = waiting.pop(0)
                job()
                if key[0] == "Z":
                    for g in range(key[3], key[4]):
                        dz_made.add((key[1], key[2], g))
                else:
                    taps_made[key[1], key[3]] = key[2]
                passes()

        loads = list(LOADS)
        for i, step in enumerate(STEPS):
            while loads and loads[0][0] <= i:
                load(*loads.pop(0)[1])
            kind, h = step[:2]
            late = i >= len(STEPS) - TAIL
            if kind == "T":
                for g in range(G):
                    if (h, step[2], g) in PE_UNITS:
                        swap_x(h, step[2], step[3], g)
                    tap_unit(h, step[2], step[3], g)
                    drain(DRAIN)
                    flush(LAG)
            else:
                dz_unit(h, step[2])
                if not late:
                    drain(DRAIN)
                flush(1)
                if late:
                    drain(DRAIN)
        flush(0)
        drain(O_CHUNKS * SLICES)
